import numpy as np
import ml_dtypes


def mxq(x, axis, fmt="e4m3"):
    dtype, down = {"e4m3": (ml_dtypes.float8_e4m3fn, 7), "e5m2": (ml_dtypes.float8_e5m2, 14)}[fmt]
    v = np.moveaxis(np.asarray(x, np.float32).astype(ml_dtypes.bfloat16).astype(np.float64), axis, -1)
    blocks = v.reshape(v.shape[:-1] + (-1, 32))
    amax = np.abs(blocks).max(-1, keepdims=True)
    byte = np.maximum(np.where(amax > 0, np.frexp(amax)[1] - 1 + 127, 0) - down, 1)
    scale = np.exp2(byte - 127.0)
    codes = (blocks / scale).astype(np.float32).astype(dtype).astype(np.float64)
    return np.moveaxis((codes * scale).reshape(v.shape), -1, axis)


WIDE = False


def mx_kscale(k):
    if not WIDE:
        return np.ones(k)
    levels = np.array([10, -10, 5, -5, 0])
    if k % 512:
        return np.exp2(np.random.permutation(np.resize(levels, k // 32))).repeat(32)
    a = np.empty((k // 512, 16))
    for p in range(k // 512):
        a[p, :8] = np.random.permutation(np.resize(levels, 8))
        for g in range(8):
            far = levels[np.abs(levels - a[p, g]) >= 10]
            a[p, g + 8] = far[np.random.randint(len(far))]
    return np.exp2(a.ravel()).repeat(32)


BF16 = ml_dtypes.bfloat16


def bf(x):
    return np.asarray(x, np.float32).astype(BF16)


def f64(x):
    return np.asarray(x).astype(np.float64)


E2M1 = np.array([0.0, 0.5, 1.0, 1.5, 2.0, 3.0, 4.0, 6.0, -0.0, -0.5, -1.0, -1.5, -2.0, -3.0, -4.0, -6.0])


def pack_weight(w, fmt):
    k, n = w.shape
    w = f64(bf(w)).reshape(k // 32, 32, n)
    amax = np.abs(w).max(1)
    if fmt == "e4m3":
        byte = np.frexp(amax)[1] - 1 + 127 - 7
    else:
        mant, ex = np.frexp(amax / 6.0)
        byte = np.where(mant > 0.5, ex, ex - 1) + 127
    byte = np.clip(np.where(amax > 0, byte, 1), 1, 254)
    scaled = (w * np.exp2(127.0 - byte)[:, None, :]).reshape(k, n).astype(np.float32)
    by_word = np.ascontiguousarray(scaled.reshape(k // 512, 128, 4, n).transpose(0, 1, 3, 2))
    if fmt == "e4m3":
        words = by_word.astype(ml_dtypes.float8_e4m3fn).view(np.uint8)
    else:
        c = by_word.astype(ml_dtypes.float4_e2m1fn).view(np.uint8) & 0xF
        words = c[..., 0::2] | (c[..., 1::2] << 4)
    return np.ascontiguousarray(words), np.ascontiguousarray(byte.astype(np.uint8).reshape(k // 512, 16, n))


def unpack_weight(words, scales, fmt):
    g, p, n, _ = words.shape
    if fmt == "e4m3":
        vals = np.ascontiguousarray(words).view(ml_dtypes.float8_e4m3fn).astype(np.float64)
    else:
        nib = np.empty((g, p, n, 4), np.uint8)
        nib[..., 0::2] = words & 0xF
        nib[..., 1::2] = words >> 4
        vals = E2M1[nib]
    vals = vals * np.repeat(np.exp2(scales.astype(np.float64) - 127.0), 8, axis=1)[..., None]
    return vals.transpose(0, 1, 3, 2).reshape(g * 512, n)


B, S, D, C, M, H = 4, 256, 1024, 16, 512, 4
LN_EPS = 1e-5


def sigmoid(v):
    return 1.0 / (1.0 + np.exp(-v))


def draw0():
    s = mx_kscale(M)
    t = mx_kscale(M)
    u = mx_kscale(M)
    g = np.concatenate([np.ones(D), u])
    x = bf(np.random.standard_normal((B, S, D)))
    query = bf(np.random.standard_normal((B, S, M)) * u)
    ctx = bf(np.random.standard_normal((B, S, M)) * 0.5 * s)
    attn_out_w = np.random.standard_normal((M, M)) * 2.0 / np.sqrt(M) * t[:, None] / s[None, :]
    attn_out_w_words, attn_out_w_scales = pack_weight(attn_out_w.T, "e4m3")
    attn_out_b = bf(np.random.standard_normal(M) * 0.3 * t)
    op_w = np.random.standard_normal((D, M)) / np.sqrt(M) / t[None, :]
    op_w_words, op_w_scales = pack_weight(op_w.T, "e4m3")
    op_b = bf(np.random.standard_normal(D) * 0.3 + 0.3)
    gate_w = np.random.standard_normal((D, D + M)) / np.sqrt(D + M) / g[None, :]
    gate_w_words, gate_w_scales = pack_weight(gate_w.T, "e4m3")
    return {
        "x": x,
        "query": query,
        "ctx": ctx,
        "attn_out_w_words": attn_out_w_words,
        "attn_out_w_scales": attn_out_w_scales,
        "attn_out_b": attn_out_b,
        "op_w_words": op_w_words,
        "op_w_scales": op_w_scales,
        "op_b": op_b,
        "gate_w_words": gate_w_words,
        "gate_w_scales": gate_w_scales,
        "gate_b": bf(np.random.standard_normal(D) * 0.5),
        "ln_g": bf(1.0 + 0.1 * np.random.standard_normal(D)),
        "ln_b": bf(0.1 * np.random.standard_normal(D)),
    }


def core(x, query, ctx, attn_out_w_words, attn_out_w_scales, attn_out_b, op_w_words, op_w_scales, op_b, gate_w_words, gate_w_scales, gate_b, ln_g, ln_b):
    x = f64(x)
    r = (mxq(f64(ctx), 2, "e4m3") @ unpack_weight(attn_out_w_words, attn_out_w_scales, "e4m3")) + f64(attn_out_b)
    retrieved = (mxq(r, 2, "e4m3") @ unpack_weight(op_w_words, op_w_scales, "e4m3")) + f64(op_b)
    gate_in = np.concatenate([x, f64(query)], axis=-1)
    gate = sigmoid((mxq(gate_in, 2, "e4m3") @ unpack_weight(gate_w_words, gate_w_scales, "e4m3")) + f64(gate_b))
    y = gate * x + (1.0 - gate) * retrieved
    mu = y.mean(axis=-1, keepdims=True)
    var = y.var(axis=-1, keepdims=True)
    return (y - mu) / np.sqrt(var + LN_EPS) * f64(ln_g) + f64(ln_b)


def e4m3fn_bytes(y):
    return np.clip(np.asarray(y, np.float64), -448.0, 448.0).astype(np.float32).astype(ml_dtypes.float8_e4m3fn).view(np.uint8)


def e4m3fn_values(b):
    return np.asarray(b, np.uint8).view(ml_dtypes.float8_e4m3fn).astype(np.float64)


def setup_inputs():
    d = draw0()
    x0 = np.asarray(d['query']).astype(np.float64)
    s = (np.max(np.abs(x0), axis=(0, 1), keepdims=True) / 448.0).astype(np.float32)
    out = {}
    for k, v in d.items():
        if k == 'query':
            out['query_bytes'] = e4m3fn_bytes(x0 / s.astype(np.float64))
            out['query_scale'] = s
        else:
            out[k] = v
    return out


def reference(x, query_bytes, query_scale, ctx, attn_out_w_words, attn_out_w_scales, attn_out_b, op_w_words, op_w_scales, op_b, gate_w_words, gate_w_scales, gate_b, ln_g, ln_b):
    return core(x, e4m3fn_values(query_bytes) * query_scale.astype(np.float64), ctx, attn_out_w_words, attn_out_w_scales, attn_out_b, op_w_words, op_w_scales, op_b, gate_w_words, gate_w_scales, gate_b, ln_g, ln_b)

from contextlib import ExitStack

import concourse.mybir as mybir
from concourse.masks import make_identity

F32 = mybir.dt.float32
BF16 = mybir.dt.bfloat16
I32 = mybir.dt.int32
U8 = mybir.dt.uint8
FP8 = mybir.dt.float8_e4m3fn
FP8X4 = mybir.dt.float8_e4m3fn_x4
ACT = mybir.ActivationFunctionType
ALU = mybir.AluOpType

P = 128
TOKENS = 1024
D = 1024
M = 512
TILES = TOKENS // P
PAIRS = TILES // 2
W = 2 * P
EPS = 1e-5
POOL_TILES = ()

FLOPS = 2 * TOKENS * (M * M + M * D + (D + M) * D)


def tile_rotelearningmemory_pa_w8_kernel(
    tc, x, query_bytes, query_scale, ctx,
    attn_out_w_words, attn_out_w_scales, attn_out_b,
    op_w_words, op_w_scales, op_b,
    gate_w_words, gate_w_scales, gate_b, ln_g, ln_b, out,
):
    nc = tc.nc
    x_rows = x.rearrange("b s d -> (b s) d").rearrange("(p i) d -> p i d", i=TILES)
    q_rows = query_bytes.rearrange("b s d -> (b s) d").rearrange("(p i) d -> p i d", i=TILES)
    c_rows = ctx.rearrange("b s d -> (b s) d").rearrange("(p i) d -> p i d", i=TILES)
    o_rows = out.rearrange("b s d -> (b s) d").rearrange("(p i) d -> p i d", i=TILES)

    with ExitStack() as stack:
        keep = stack.enter_context(tc.tile_pool(name="keep", bufs=1))
        work = stack.enter_context(tc.tile_pool(name="work", bufs=2))
        psum = stack.enter_context(tc.psum_pool(name="psum", bufs=8))

        x_sb = keep.tile([P, TILES, D], BF16, name="x_sb", align_bytes=64)
        c_sb = keep.tile([P, TILES, M], BF16, name="c_sb", align_bytes=64)
        q_u8 = keep.tile([P, TILES, M], U8, name="q_u8", align_bytes=64)
        q_sc = keep.tile([P, M], F32, name="q_sc")
        aw = keep.tile([P, M], I32, name="aw", align_bytes=64)
        aw_s = keep.tile([P, M], U8, name="aw_s", align_bytes=64)
        awp = keep.tile([P, M], I32, name="awp", align_bytes=64)
        awp_s = keep.tile([P, M], U8, name="awp_s", align_bytes=64)
        ow = keep.tile([P, D], I32, name="ow", align_bytes=64)
        gw = keep.tile([P, 3, D], I32, name="gw", align_bytes=64)
        go_s = keep.tile([P, D], U8, name="go_s", align_bytes=64)
        brow = keep.tile([P, P], BF16, name="brow")
        ab = keep.tile([P, 4], BF16, name="ab")
        g_bc = keep.tile([P, D], BF16, name="g_bc")
        b_bc = keep.tile([P, D], BF16, name="b_bc")
        ident32 = keep.tile([P, P], F32, name="ident32")
        ident16 = keep.tile([P, P], BF16, name="ident16")
        neg_half = keep.tile([P, 1], F32, name="neg_half")
        warm = keep.tile([P, 1], F32, name="warm")
        bcol = keep.tile([P, 16], F32, name="bcol")
        sums = keep.tile([P, 16], F32, name="sums")
        nm = keep.tile([P, 8], F32, name="nm")
        ssq = keep.tile([P, 8], F32, name="ssq")
        var = keep.tile([P, 8], F32, name="var")
        rstd = keep.tile([P, 8], F32, name="rstd")
        nmr = keep.tile([P, 8], F32, name="nmr")

        nc.vector.memset(warm[:], 0.0)
        nc.vector.memset(brow[:].bitcast(I32), 0)
        nc.vector.memset(aw_s[:].bitcast(I32), 0)
        nc.vector.memset(go_s[:].bitcast(I32), 0)
        make_identity(nc, ident32[:])
        make_identity(nc, ident16[:])
        nc.gpsimd.memset(neg_half[:], -0.5)
        nc.scalar.dma_start(out=q_sc[:], in_=query_scale.rearrange("a b k -> (a b k)").partition_broadcast(P))
        nc.scalar.dma_start(out=ab[:], in_=attn_out_b.rearrange("(p t) -> p t", t=4))
        nc.scalar.dma_start(out=brow[0:8, :], in_=gate_b.rearrange("(j p) -> j p", p=P))
        nc.scalar.dma_start(out=brow[8:16, :], in_=op_b.rearrange("(j p) -> j p", p=P))
        nc.scalar.activation(warm[:], warm[:], ACT.Sigmoid)

        def load(dst, src, i0, i1):
            nc.sync.dma_start(out=dst[:, i0:i1, :], in_=src[:, i0:i1, :])

        def words(dst, src):
            nc.sync.dma_start(out=dst, in_=src.rearrange("p n t -> p (n t)").bitcast(I32))

        load(c_sb, c_rows, 0, 2)
        load(q_u8, q_rows, 0, 4)
        words(aw[:], attn_out_w_words[0])
        for q in range(4):
            nc.sync.dma_start(out=aw_s[32 * q : 32 * q + 4, :].bitcast(I32), in_=attn_out_w_scales[0, 4 * q : 4 * q + 4, :].bitcast(I32))
        load(x_sb, x_rows, 0, 2)
        load(c_sb, c_rows, 2, 4)
        load(x_sb, x_rows, 2, 4)
        load(c_sb, c_rows, 4, 8)
        load(q_u8, q_rows, 4, 8)
        nc.sync.dma_start(out=gw[:], in_=gate_w_words.rearrange("g p n t -> p g (n t)").bitcast(I32))
        words(ow[:], op_w_words[0])
        for q in range(4):
            nc.sync.dma_start(out=go_s[32 * q : 32 * q + 12, :].bitcast(I32), in_=gate_w_scales[:, 4 * q : 4 * q + 4, :].bitcast(I32))
            nc.sync.dma_start(out=go_s[32 * q + 12 : 32 * q + 16, :].bitcast(I32), in_=op_w_scales[0, 4 * q : 4 * q + 4, :].bitcast(I32))
        load(x_sb, x_rows, 4, 6)
        load(x_sb, x_rows, 6, 8)

        cg, cc, cs = [], [], []
        qw, qg, qc, qs = [], [], [], []
        xg, xc, xs, xt = [], [], [], []
        rb, rg, rc, rs = [], [], [], []

        def bank(shape, dtype):
            t = psum.tile(shape, dtype, name="bank")
            return t

        def word_transposes(dst, rows):
            w = rows.bitcast(F32)
            for u in range(2):
                nc.tensor.transpose(dst[:, u, :], w[:, u:256:2], ident32[:])

        def ctx_t(k):
            t = bank([P, 2, 2, P], F32)
            for i in range(2):
                word_transposes(t[:, i], c_sb[:, 2 * k + i, :])
            g = work.tile([P, 2 * P * 4], BF16, name="cg", bufs=2, align_bytes=64)
            nc.scalar.copy(g[:].bitcast(F32).rearrange("p (i r u) -> p i r u", i=2, u=2), t[:].rearrange("p i u r -> p i r u"))
            cg.append(g)

        def ctx_q(k):
            c = work.tile([P, W], I32, name="cc", align_bytes=64)
            s = work.tile([P, W], U8, name="cs", align_bytes=64)
            nc.vector.quantize_mx(out=c[:].bitcast(FP8X4), scales=s[:], in_=cg[k][:])
            cc.append(c)
            cs.append(s)

        def q_w(k):
            w = work.tile([P, 2, M], BF16, name="qw", align_bytes=64)
            for i in range(2):
                nc.vector.tensor_tensor(w[:, i, :], q_u8[:, 2 * k + i, :].bitcast(FP8), q_sc[:], ALU.mult)
            qw.append(w)

        def q_t(k):
            t = bank([P, 2, 2, P], F32)
            for i in range(2):
                word_transposes(t[:, i], qw[k][:, i, :])
            g = work.tile([P, 2 * P * 4], BF16, name="qg", align_bytes=64)
            nc.scalar.copy(g[:].bitcast(F32).rearrange("p (i r u) -> p i r u", i=2, u=2), t[:].rearrange("p i u r -> p i r u"))
            qg.append(g)

        def q_q(k):
            c = work.tile([P, W], I32, name="qc", bufs=4, align_bytes=64)
            s = work.tile([P, W], U8, name="qs", bufs=4, align_bytes=64)
            nc.vector.quantize_mx(out=c[:].bitcast(FP8X4), scales=s[:], in_=qg[k][:])
            qc.append(c)
            qs.append(s)

        def x_t(k):
            g = work.tile([P, 2, W * 4], BF16, name="xg", align_bytes=64)
            gv = g[:].bitcast(F32).rearrange("p g (i r u) -> p g i r u", i=2, u=2)
            for i in range(2):
                t = bank([P, 2, 2, P], F32)
                for h in range(2):
                    word_transposes(t[:, h], x_sb[:, 2 * k + i, h * 512 : (h + 1) * 512])
                nc.scalar.copy(gv[:, :, i], t[:].rearrange("p g u r -> p g r u"))
            xg.append(g)

        def x_q(k):
            c = work.tile([P, 2, W], I32, name="xc", bufs=4, align_bytes=64)
            s = work.tile([P, 2, W], U8, name="xs", bufs=4, align_bytes=64)
            nc.vector.quantize_mx(
                out=c[:].rearrange("p g w -> p (g w)").bitcast(FP8X4),
                scales=s[:].rearrange("p g w -> p (g w)"),
                in_=xg[k][:].rearrange("p g w -> p (g w)"),
            )
            xc.append(c)
            xs.append(s)

        def xt_t(k):
            dst = work.tile([P, 8, W], BF16, name="xt", bufs=4)
            for i in range(2):
                for h in range(2):
                    t = bank([P, 4, P], BF16)
                    for j in range(4):
                        d0 = (4 * h + j) * P
                        nc.tensor.transpose(t[:, j, :], x_sb[:, 2 * k + i, d0 : d0 + P], ident16[:])
                    nc.scalar.copy(dst[:, 4 * h : 4 * h + 4, i * P : (i + 1) * P], t[:])
            xt.append(dst)

        def r_mm(k):
            banks = []
            for i in range(2):
                t = bank([P, 4, P], F32)
                for j in range(4):
                    nc.tensor.matmul_mx(
                        out=t[:, j, :],
                        lhsT=awp[:, j * P : (j + 1) * P].bitcast(FP8X4),
                        lhsT_scale=awp_s[:, j * P : (j + 1) * P],
                        rhs=cc[k][:, i * P : (i + 1) * P].bitcast(FP8X4),
                        rhs_scale=cs[k][:, i * P : (i + 1) * P],
                        start=True,
                        stop=True,
                    )
                banks.append(t)
            rb.append(banks)

        def r_ev(k):
            g = work.tile([P, 2, P, 4], BF16, name="rg", align_bytes=64)
            for i in range(2):
                nc.vector.tensor_tensor(
                    g[:, i],
                    rb[k][i][:].rearrange("p t r -> p r t"),
                    ab[:].unsqueeze(1).to_broadcast([P, P, 4]),
                    ALU.add,
                )
            rg.append(g)

        def r_q(k):
            c = work.tile([P, W], I32, name="rc", bufs=4, align_bytes=64)
            s = work.tile([P, W], U8, name="rs", bufs=4, align_bytes=64)
            nc.vector.quantize_mx(out=c[:].bitcast(FP8X4), scales=s[:], in_=rg[k][:].rearrange("p i r t -> p (i r t)"))
            rc.append(c)
            rs.append(s)

        def permute():
            nc.vector.tensor_copy(awp[:].rearrange("p (t m) -> p t m", t=4), aw[:].rearrange("p (m t) -> p t m", t=4))
            nc.vector.tensor_copy(awp_s[:].rearrange("p (t m) -> p t m", t=4), aw_s[:].rearrange("p (m t) -> p t m", t=4))

        def biases():
            t = bank([P, P], BF16)
            nc.tensor.transpose(t[:], brow[:], ident16[:])
            nc.scalar.mul(bcol[:, 0:8], t[:, 0:8], -1.0)
            nc.scalar.copy(bcol[:, 8:16], t[:, 8:16])

        gbk, rbk, gt, dt_, mt, yb, ysb = {}, {}, {}, {}, {}, {}, {}

        def mx(s):
            k, h = divmod(s, 2)
            gbk[s], rbk[s] = [], []
            for jj in range(2):
                t = bank([P, 2, W], F32)
                for j in range(2):
                    c0 = (4 * h + 2 * jj + j) * P
                    nc.tensor.matmul_mx(
                        out=t[:, j, :], lhsT=ow[:, c0 : c0 + P].bitcast(FP8X4), lhsT_scale=go_s[12:P, c0 : c0 + P],
                        rhs=rc[k][:].bitcast(FP8X4), rhs_scale=rs[k][:], start=True, stop=True,
                    )
                rbk[s].append(t)
                t2 = bank([P, 2, W], F32)
                for j in range(2):
                    c0 = (4 * h + 2 * jj + j) * P
                    for g in range(3):
                        codes = qc[k][:] if g == 2 else xc[k][:, g, :]
                        scales = qs[k][:] if g == 2 else xs[k][:, g, :]
                        nc.tensor.matmul_mx(
                            out=t2[:, j, :], lhsT=gw[:, g, c0 : c0 + P].bitcast(FP8X4), lhsT_scale=go_s[4 * g : P, c0 : c0 + P],
                            rhs=codes.bitcast(FP8X4), rhs_scale=scales, start=(g == 0), stop=(g == 2),
                        )
                gbk[s].append(t2)

        def sig(s):
            h = s % 2
            t = work.tile([P, 4, W], F32, name="gt")
            for j in range(4):
                col = 4 * h + j
                nc.scalar.activation(t[:, j, :], gbk[s][j // 2][:, j % 2, :], ACT.Sigmoid, bias=bcol[:, col : col + 1], scale=-1.0)
            gt[s] = t

        def diff(s):
            k, h = divmod(s, 2)
            t = work.tile([P, 4, W], F32, name="dt")
            for j in range(4):
                col = 4 * h + j
                nc.vector.scalar_tensor_tensor(
                    t[:, j, :], rbk[s][j // 2][:, j % 2, :], bcol[:, 8 + col : 9 + col], xt[k][:, col, :], ALU.add, ALU.subtract
                )
            dt_[s] = t

        def prod(s):
            t = work.tile([P, 4, W], F32, name="mt")
            nc.vector.tensor_tensor(t[:], gt[s][:], dt_[s][:], ALU.mult)
            mt[s] = t

        def y_mm(s):
            k, h = divmod(s, 2)
            yb[s] = []
            for i in range(2):
                t = bank([P, 4, P], F32)
                nc.tensor.matmul(t[:].rearrange("p j d -> p (j d)"), lhsT=ident16[:], rhs=x_sb[:, 2 * k + i, h * 512 : (h + 1) * 512], start=True, stop=False)
                for j in range(4):
                    nc.tensor.matmul(t[:, j, :], lhsT=mt[s][:, j, i * P : (i + 1) * P], rhs=ident32[:], start=False, stop=(j == 3), is_transpose=True)
                yb[s].append(t)

        def y_ev(s):
            k, h = divmod(s, 2)
            if h == 0:
                ysb[k] = work.tile([P, 2, D], F32, name="ysb", bufs=3)
            for i in range(2):
                c = 2 * (2 * k + i) + h
                nc.scalar.activation(ysb[k][:, i, h * 512 : (h + 1) * 512], yb[s][i][:].rearrange("p j d -> p (j d)"), ACT.Identity, accum_out=sums[:, c : c + 1])

        def means(k):
            for c in (2 * k, 2 * k + 1):
                nc.gpsimd.tensor_scalar(nm[:, c : c + 1], sums[:, 2 * c : 2 * c + 1], sums[:, 2 * c + 1 : 2 * c + 2], -1.0 / D, ALU.add, ALU.mult)

        def squares(c):
            if c < 0:
                return
            junk = work.tile([P, D], BF16, name="junk")
            nc.scalar.activation(junk[:], ysb[c // 2][:, c % 2, :], ACT.Square, bias=nm[:, c : c + 1], accum_out=ssq[:, c : c + 1])
            nc.gpsimd.tensor_scalar(var[:, c : c + 1], ssq[:, c : c + 1], 1.0 / D, EPS, ALU.mult, ALU.add)
            nc.gpsimd.tensor_tensor(rstd[:, c : c + 1], var[:, c : c + 1], neg_half[:], ALU.pow)
            if c in POOL_TILES:
                nc.gpsimd.tensor_tensor(nmr[:, c : c + 1], nm[:, c : c + 1], rstd[:, c : c + 1], ALU.mult)

        tt = {}

        def ln_n(c):
            k, i = divmod(c, 2)
            n = work.tile([P, D], F32, name="nt", bufs=2)
            nc.scalar.activation(n[:], ysb[k][:, i, :], ACT.Identity, bias=nmr[:, c : c + 1], scale=rstd[:, c : c + 1])
            tt[c] = n

        def pool_gb(c):
            n = tt[c]
            o = work.tile([P, D], F32, name="og", bufs=2)
            for q in range(0, D, 256):
                nc.gpsimd.tensor_tensor(o[:, q : q + 256], n[:, q : q + 256], g_bc[:, q : q + 256], ALU.mult)
            for q in range(0, D, 256):
                nc.gpsimd.tensor_tensor(o[:, q : q + 256], o[:, q : q + 256], b_bc[:, q : q + 256], ALU.add)
            nc.sync.dma_start(out=o_rows[:, c, :], in_=o[:])

        def ln1(c):
            k, i = divmod(c, 2)
            t = work.tile([P, D], F32, name="lt", bufs=4)
            nc.vector.scalar_tensor_tensor(t[:], ysb[k][:, i, :], nm[:, c : c + 1], g_bc[:], ALU.add, ALU.mult)
            tt[c] = t

        def ln2(c):
            o = work.tile([P, D], F32, name="ot", bufs=3)
            nc.vector.scalar_tensor_tensor(o[:], tt[c][:], rstd[:, c : c + 1], b_bc[:], ALU.mult, ALU.add)
            nc.sync.dma_start(out=o_rows[:, c, :], in_=o[:])

        PRE = {0: (), 1: (), 2: (0, 1,), 3: (), 4: (2, 3,), 5: (), 6: (4, 5,), 7: ()}
        MID = {0: (), 1: (), 2: (), 3: (0, 1,), 4: (), 5: (2, 3,), 6: (), 7: (4, 5,)}
        LAST = (6, 7)
        S = 2 * PAIRS

        ctx_t(0)
        q_w(0)
        biases()
        permute()
        ctx_q(0)
        q_t(0)
        q_w(1)
        x_t(0)
        r_mm(0)
        q_q(0)
        r_ev(0)
        ctx_t(1)
        ctx_q(1)
        q_t(1)
        r_q(0)
        r_mm(1)
        x_q(0)
        q_w(2)
        xt_t(0)
        ctx_t(2)
        r_ev(1)
        q_q(1)
        x_t(1)
        ctx_q(2)
        r_mm(2)
        r_q(1)
        q_t(2)
        x_q(1)
        xt_t(1)
        q_w(3)
        r_ev(2)
        ctx_t(3)
        q_q(2)
        nc.scalar.dma_start(out=g_bc[:], in_=ln_g.partition_broadcast(P))
        nc.scalar.dma_start(out=b_bc[:], in_=ln_b.partition_broadcast(P))
        mx(0)
        sig(0)
        ctx_q(3)
        q_t(3)
        r_q(2)
        r_mm(3)
        q_q(3)
        r_ev(3)
        r_q(3)
        for s in range(S):
            k, h = divmod(s, 2)
            if s == 0:
                x_t(2)
            if s == 1:
                xt_t(2)
            if s == 2:
                x_t(3)
            if s == 3:
                xt_t(3)
            if s + 1 < S:
                mx(s + 1)
            diff(s)
            if s + 1 < S:
                sig(s + 1)
            if h == 0:
                squares(2 * k - 2)
            for c in MID[s]:
                ln2(c)
            if s == 1:
                x_q(2)
            if s == 3:
                x_q(3)
            prod(s)
            y_mm(s)
            y_ev(s)
            if h == 0:
                squares(2 * k - 1)
            if h == 1:
                means(k)
            for c in PRE[s]:
                if c in POOL_TILES:
                    ln_n(c)
                    pool_gb(c)
                else:
                    ln1(c)
        squares(6)
        squares(7)
        for c in LAST:
            ln1(c)
        for c in LAST:
            ln2(c)
